import numpy as np
import ml_dtypes


def mxq(x, axis, fmt="e4m3"):
    dtype, down = {"e4m3": (ml_dtypes.float8_e4m3fn, 7), "e5m2": (ml_dtypes.float8_e5m2, 14)}[fmt]
    v = np.moveaxis(np.asarray(x, np.float32).astype(ml_dtypes.bfloat16).astype(np.float64), axis, -1)
    blocks = v.reshape(v.shape[:-1] + (-1, 32))
    amax = np.abs(blocks).max(-1, keepdims=True)
    byte = np.maximum(np.where(amax > 0, np.frexp(amax)[1] - 1 + 127, 0) - down, 1)
    scale = np.exp2(byte - 127.0)
    codes = (blocks / scale).astype(np.float32).astype(dtype).astype(np.float64)
    return np.moveaxis((codes * scale).reshape(v.shape), -1, axis)


WIDE = False


def mx_kscale(k):
    if not WIDE:
        return np.ones(k)
    levels = np.array([10, -10, 5, -5, 0])
    a = np.random.permutation(np.resize(levels, k // 512 * 4)).reshape(k // 512, 4)
    idx = np.arange(k)
    return np.exp2(a[idx // 512, idx % 128 // 32])


BF16 = ml_dtypes.bfloat16


def bf(x):
    return np.asarray(x, np.float32).astype(BF16)


def f64(x):
    return np.asarray(x).astype(np.float64)


E2M1 = np.array([0.0, 0.5, 1.0, 1.5, 2.0, 3.0, 4.0, 6.0, -0.0, -0.5, -1.0, -1.5, -2.0, -3.0, -4.0, -6.0])


def pack_weight(w, fmt):
    k, n = w.shape
    w = f64(bf(w)).reshape(k // 32, 32, n)
    amax = np.abs(w).max(1)
    if fmt == "e4m3":
        byte = np.frexp(amax)[1] - 1 + 127 - 7
    else:
        mant, ex = np.frexp(amax / 6.0)
        byte = np.where(mant > 0.5, ex, ex - 1) + 127
    byte = np.clip(np.where(amax > 0, byte, 1), 1, 254)
    scaled = (w * np.exp2(127.0 - byte)[:, None, :]).reshape(k, n).astype(np.float32)
    by_word = np.ascontiguousarray(scaled.reshape(k // 512, 128, 4, n).transpose(0, 1, 3, 2))
    if fmt == "e4m3":
        words = by_word.astype(ml_dtypes.float8_e4m3fn).view(np.uint8)
    else:
        c = by_word.astype(ml_dtypes.float4_e2m1fn).view(np.uint8) & 0xF
        words = c[..., 0::2] | (c[..., 1::2] << 4)
    return np.ascontiguousarray(words), np.ascontiguousarray(byte.astype(np.uint8).reshape(k // 512, 16, n))


def unpack_weight(words, scales, fmt):
    g, p, n, _ = words.shape
    if fmt == "e4m3":
        vals = np.ascontiguousarray(words).view(ml_dtypes.float8_e4m3fn).astype(np.float64)
    else:
        nib = np.empty((g, p, n, 4), np.uint8)
        nib[..., 0::2] = words & 0xF
        nib[..., 1::2] = words >> 4
        vals = E2M1[nib]
    vals = vals * np.repeat(np.exp2(scales.astype(np.float64) - 127.0), 8, axis=1)[..., None]
    return vals.transpose(0, 1, 3, 2).reshape(g * 512, n)

def pack4(w):
    words, scales = pack_weight(w, "e2m1")
    return words.reshape(words.shape[0], 128, -1), scales


def unpack4(words, scales):
    return unpack_weight(words.reshape(words.shape[0], 128, -1, 2), scales, "e2m1")


B, T, C, N_HEAD, N_KV, HD, WINDOW = 1, 4096, 1024, 4, 2, 128, 512
QPK = N_HEAD // N_KV
TOT = QPK + 2
QKV_OUT = N_KV * TOT * HD


def apply_rope(xh, fc):
    b, t, h, d = xh.shape
    xs = xh.reshape(b, t, h, d // 2, 2)
    f = fc.reshape(1, t, 1, d // 2, 2)
    re = xs[..., 0] * f[..., 0] - xs[..., 1] * f[..., 1]
    im = xs[..., 1] * f[..., 0] + xs[..., 0] * f[..., 1]
    return np.stack([re, im], axis=-1).reshape(b, t, h, d)


def setup_inputs():
    s = mx_kscale(C)
    inv_freq = 1.0 / (10000.0 ** (np.arange(0, HD, 2) / HD))
    ang = np.outer(np.arange(T), inv_freq)
    x = bf(np.random.standard_normal((B, T, C)) * s)
    freqs_cis = bf(np.stack([np.cos(ang), np.sin(ang)], axis=-1))
    words, scales = pack4(np.random.standard_normal((C, QKV_OUT)) * 1.5 / np.sqrt(C) / s[:, None])
    return {"x": x,
            "freqs_cis": freqs_cis,
            "W_attn_words": words,
            "W_attn_scales": scales}


def reference(x, freqs_cis, W_attn_words, W_attn_scales):
    qkv = mxq(f64(x), 2, "e4m3") @ unpack4(W_attn_words, W_attn_scales)
    qkv = qkv.reshape(B, T, N_KV, TOT, HD).transpose(0, 2, 3, 1, 4)
    q = qkv[:, :, :QPK].reshape(B, -1, N_HEAD, HD)
    k = qkv[:, :, QPK:QPK + 1].reshape(B, -1, N_KV, HD)
    v = qkv[:, :, QPK + 1:].reshape(B, -1, N_KV, HD)
    fc = f64(freqs_cis)
    return apply_rope(q, fc), apply_rope(k, fc), v

@@ -1,0 +1,236 @@
+from contextlib import ExitStack
+
+import concourse.mybir as mybir
+from concourse.masks import make_identity
+
+FLOPS = 2 * 4096 * 1024 * 1024
+
+F32 = mybir.dt.float32
+BF16 = mybir.dt.bfloat16
+I32 = mybir.dt.int32
+U32 = mybir.dt.uint32
+U8 = mybir.dt.uint8
+FP8X4 = mybir.dt.float8_e4m3fn_x4
+FP4X4 = mybir.dt.float4_e2m1fn_x4
+MULT = mybir.AluOpType.mult
+ADD = mybir.AluOpType.add
+
+P = 128
+TOKENS = 4096
+C = 1024
+HEAD = 128
+PAIRS = HEAD // 2
+GROUPS = 2
+PACK = 4
+K_PASS = P * PACK
+PASSES = C // K_PASS
+PASS_WORDS = K_PASS // 2
+CHUNK = 4
+CHUNKS = TOKENS // (P * CHUNK)
+ROUNDS = 2 * CHUNKS
+Q_BLOCKS = 4
+ROTATED = Q_BLOCKS + GROUPS
+Q_COLS = Q_BLOCKS * HEAD
+
+
+def tile_causalselfattentiongqa_pa_t_kernel(
+    tc, x, freqs_cis, W_attn_words, W_attn_scales, out_0, out_1, out_2
+):
+    nc = tc.nc
+
+    x_rows = x.rearrange("o (p r) k -> p (o r) k", p=P)
+    table_q = freqs_cis.rearrange("(b p c) i e -> p b c i e", b=Q_BLOCKS, p=P)
+    table_k = freqs_cis.rearrange("(g p r) i e -> p g r i e", g=GROUPS, p=P)
+    q_rows = out_0.rearrange("o n h f -> (o n h) f").rearrange("(b p r) f -> p b r f", b=Q_BLOCKS, p=P)
+    k_rows = out_1.rearrange("o n h f -> (o n h) f").rearrange("(g p r) f -> p g r f", g=GROUPS, p=P)
+    v_rows = out_2.rearrange("o n h f -> (o n h) f").rearrange("(g p r) f -> p g r f", g=GROUPS, p=P)
+    w_words = W_attn_words.bitcast(I32).rearrange("h p (g s w) -> h p g s w", g=GROUPS, s=4)
+    w_scale_rows = W_attn_scales.bitcast(I32).rearrange("h (q r) w -> r q h w", r=4)
+
+    with ExitStack() as ctx:
+        ctx.enter_context(tc.manual_schedule())
+        consts = ctx.enter_context(tc.tile_pool(name="consts", bufs=1))
+        x_pool = ctx.enter_context(tc.tile_pool(name="x_pool", bufs=ROUNDS))
+        table_pool = ctx.enter_context(tc.tile_pool(name="table_pool", bufs=CHUNKS))
+        stage = ctx.enter_context(tc.tile_pool(name="stage", bufs=3))
+        outs = ctx.enter_context(tc.tile_pool(name="outs", bufs=4))
+        psum_xt = ctx.enter_context(tc.psum_pool(name="psum_xt", bufs=2))
+        psum_q = ctx.enter_context(tc.psum_pool(name="psum_q", bufs=3))
+        psum_k = ctx.enter_context(tc.psum_pool(name="psum_k", bufs=2))
+        psum_v = ctx.enter_context(tc.psum_pool(name="psum_v", bufs=1))
+
+        ident = consts.tile([P, P], F32)
+        make_identity(nc, ident[:])
+
+        wq_words = consts.tile([P, PASSES, 2 * Q_COLS], U8, align_bytes=64)
+        wkv_words = consts.tile([P, PASSES, 2 * Q_COLS], U8, align_bytes=64)
+        w_scales = consts.tile([P, PASSES, C], U8, align_bytes=64)
+        wq_scales = consts.tile([P, PASSES, Q_COLS], U8, align_bytes=64)
+        nc.vector.memset(w_scales[:].bitcast(I32), 0)
+
+        def load_round(i):
+            c, r = divmod(i, 2)
+            x_tile = x_pool.tile([P, 2, C], BF16)
+            nc.sync.dma_start(out=x_tile[:], in_=x_rows[:, CHUNK * c + r : CHUNK * (c + 1) : 2, :])
+            return x_tile
+
+        def load_weight():
+            for r in range(4):
+                nc.sync.dma_start(out=w_scales[r:P:32, :, :].bitcast(I32), in_=w_scale_rows[r])
+            for h in range(PASSES):
+                nc.sync.dma_start(
+                    out=wq_words[:, h, :].bitcast(I32).rearrange("p (g s w) -> p g s w", g=GROUPS, s=2),
+                    in_=w_words[h][:, :, 0:2, :],
+                )
+                nc.sync.dma_start(
+                    out=wkv_words[:, h, :].bitcast(I32).rearrange("p (g s w) -> p g s w", g=GROUPS, s=2),
+                    in_=w_words[h][:, :, 2:4, :],
+                )
+
+        def gather_query_scales():
+            by_group = w_scales[:].bitcast(I32).rearrange("p h (g w) -> p h g w", g=GROUPS)
+            nc.vector.tensor_copy(
+                out=wq_scales[:].bitcast(I32).rearrange("p h (g w) -> p h g w", g=GROUPS),
+                in_=by_group[:, :, :, 0 : Q_COLS // GROUPS // 4],
+            )
+
+        def load_tables(c):
+            q_table = table_pool.tile([P, Q_BLOCKS, 1, PAIRS, 2], BF16)
+            nc.sync.dma_start(out=q_table[:], in_=table_q[:, :, c : c + 1, :, :])
+            k_table = table_pool.tile([P, GROUPS, 2, PAIRS, 2], BF16)
+            nc.sync.dma_start(out=k_table[:], in_=table_k[:, :, 2 * c : 2 * c + 2, :, :])
+            return q_table, k_table
+
+        def transpose_round(x_tile):
+            words = x_tile[:].bitcast(F32)
+            grouped = stage.tile([P, 2, PASSES, P, PACK], BF16, align_bytes=64)
+            for t in range(2):
+                xt = psum_xt.tile([P, PASSES, 2, P], F32)
+                for h in range(PASSES):
+                    for u in range(2):
+                        nc.tensor.transpose(
+                            xt[:, h, u, :],
+                            words[:, t, PASS_WORDS * h + u : PASS_WORDS * (h + 1) : 2],
+                            ident[:],
+                        )
+                nc.scalar.copy(out=grouped[:, t].bitcast(F32), in_=xt[:].rearrange("p h u n -> p h n u"))
+            return grouped
+
+        def quantise(grouped):
+            codes = stage.tile([P, 2 * PASSES * P], U32, align_bytes=64)
+            scales = stage.tile([P, 2 * PASSES * P], U8, align_bytes=64)
+            nc.vector.quantize_mx(
+                out=codes[:].bitcast(FP8X4),
+                scales=scales[:],
+                in_=grouped[:].rearrange("p t h n k -> p (t h n k)"),
+            )
+            return codes, scales
+
+        def multiply(acc, operand, t, weight_words, weight_scales):
+            codes, scales = operand
+            for h in range(PASSES):
+                cols = slice((PASSES * t + h) * P, (PASSES * t + h + 1) * P)
+                nc.tensor.matmul_mx(
+                    out=acc,
+                    lhsT=codes[:, cols].bitcast(FP8X4),
+                    lhsT_scale=scales[:, cols],
+                    rhs=weight_words(h).bitcast(FP4X4),
+                    rhs_scale=weight_scales(h),
+                    start=(h == 0),
+                    stop=(h == PASSES - 1),
+                )
+
+        def project(operand):
+            q_banks = []
+            for t in range(2):
+                q_bank = psum_q.tile([P, Q_COLS], F32)
+                multiply(q_bank[:], operand, t, lambda h: wq_words[:, h, :], lambda h: wq_scales[:, h, :])
+                q_banks.append(q_bank)
+            k_bank = psum_k.tile([P, GROUPS, 2, HEAD], F32)
+            v_bank = psum_v.tile([P, GROUPS, 2, HEAD], F32)
+            for s, bank in ((0, k_bank), (1, v_bank)):
+                for g in range(GROUPS):
+                    kv = 2 * g + s
+                    col = (4 * g + 2 + s) * HEAD
+                    for t in range(2):
+                        multiply(
+                            bank[:, g, t, :],
+                            operand,
+                            t,
+                            lambda h: wkv_words[:, h, 2 * HEAD * kv : 2 * HEAD * (kv + 1)],
+                            lambda h: w_scales[:, h, col : col + HEAD],
+                        )
+            return q_banks, k_bank, v_bank
+
+        def rotate_bank(bank, table, straight, cross):
+            cos = table[:, :, :, :, 0:1].to_broadcast(list(bank.shape))
+            sin = table[:, :, :, :, 1]
+            nc.vector.tensor_tensor(out=straight, in0=bank, in1=cos, op=MULT)
+            nc.vector.scalar_tensor_tensor(
+                out=cross[:, 0], in0=bank[:, :, :, :, 1], scalar=-1.0, in1=sin, op0=MULT, op1=MULT
+            )
+            nc.vector.tensor_tensor(out=cross[:, 1], in0=bank[:, :, :, :, 0], in1=sin, op=MULT)
+
+        def rotate(banks, tables):
+            q_banks, k_bank, v_bank = banks
+            q_table, k_table = tables
+            straight = stage.tile([P, ROTATED, 2, PAIRS, 2], F32)
+            cross = stage.tile([P, 2, ROTATED, 2, PAIRS], F32)
+            for t in range(2):
+                rotate_bank(
+                    q_banks[t][:].rearrange("p (b o i e) -> p b o i e", b=Q_BLOCKS, o=1, e=2),
+                    q_table[:],
+                    straight[:, 0:Q_BLOCKS, t : t + 1, :, :],
+                    cross[:, :, 0:Q_BLOCKS, t : t + 1, :],
+                )
+            rotate_bank(
+                k_bank[:].rearrange("p g t (i e) -> p g t i e", e=2),
+                k_table[:],
+                straight[:, Q_BLOCKS:ROTATED, :, :, :],
+                cross[:, :, Q_BLOCKS:ROTATED, :, :],
+            )
+            return straight, cross
+
+        x_tiles = [load_round(0), load_round(1)]
+        load_weight()
+        tables = [load_tables(0)]
+        for c in range(1, CHUNKS):
+            x_tiles.append(load_round(2 * c))
+            x_tiles.append(load_round(2 * c + 1))
+            tables.append(load_tables(c))
+
+        operands = {0: quantise(transpose_round(x_tiles[0]))}
+        gather_query_scales()
+        operands[1] = quantise(transpose_round(x_tiles[1]))
+        banks = {0: project(operands[0])}
+        qk_out = None
+        v_out = None
+        for i in range(ROUNDS):
+            c, r = divmod(i, 2)
+            if r == 0:
+                qk_out = outs.tile([P, ROTATED, 2, 2, PAIRS, 2], F32)
+                v_out = outs.tile([P, GROUPS, 2, 2, HEAD], F32)
+            nc.scalar.copy(out=v_out[:, :, :, r, :], in_=banks[i][2][:])
+            straight, cross = rotate(banks[i], tables[c])
+            grouped = transpose_round(x_tiles[i + 2]) if i + 2 < ROUNDS else None
+            if i + 1 < ROUNDS:
+                banks[i + 1] = project(operands[i + 1])
+            if i + 2 < ROUNDS:
+                operands[i + 2] = quantise(grouped)
+            nc.gpsimd.tensor_tensor(
+                out=qk_out[:, :, :, r, :, :],
+                in0=straight[:],
+                in1=cross[:].rearrange("p e b t i -> p b t i e"),
+                op=ADD,
+            )
+            if r == 1:
+                rows = slice(CHUNK * c, CHUNK * (c + 1))
+                nc.sync.dma_start(out=v_rows[:, :, rows, :], in_=v_out[:].rearrange("p g t r f -> p g (t r) f"))
+                nc.sync.dma_start(
+                    out=q_rows[:, :, rows, :],
+                    in_=qk_out[:, 0:Q_BLOCKS].rearrange("p b t r i e -> p b (t r) (i e)"),
+                )
+                nc.sync.dma_start(
+                    out=k_rows[:, :, rows, :],
+                    in_=qk_out[:, Q_BLOCKS:ROTATED].rearrange("p b t r i e -> p b (t r) (i e)"),
+                )

@@ -31,6 +31,7 @@ ROUNDS = 2 * CHUNKS
 Q_BLOCKS = 4
 ROTATED = Q_BLOCKS + GROUPS
 Q_COLS = Q_BLOCKS * HEAD
+TABLE_ROWS = Q_BLOCKS + 2 * GROUPS
 
 
 def tile_causalselfattentiongqa_pa_t_kernel(
@@ -52,7 +53,9 @@ def tile_causalselfattentiongqa_pa_t_kernel(
         consts = ctx.enter_context(tc.tile_pool(name="consts", bufs=1))
         x_pool = ctx.enter_context(tc.tile_pool(name="x_pool", bufs=ROUNDS))
         table_pool = ctx.enter_context(tc.tile_pool(name="table_pool", bufs=CHUNKS))
+        turned_pool = ctx.enter_context(tc.tile_pool(name="turned_pool", bufs=2))
         stage = ctx.enter_context(tc.tile_pool(name="stage", bufs=3))
+        operand_pool = ctx.enter_context(tc.tile_pool(name="operand_pool", bufs=4))
         outs = ctx.enter_context(tc.tile_pool(name="outs", bufs=4))
         psum_xt = ctx.enter_context(tc.psum_pool(name="psum_xt", bufs=2))
         psum_q = ctx.enter_context(tc.psum_pool(name="psum_q", bufs=3))
@@ -94,12 +97,20 @@ def tile_causalselfattentiongqa_pa_t_kernel(
                 in_=by_group[:, :, :, 0 : Q_COLS // GROUPS // 4],
             )
 
-        def load_tables(c):
-            q_table = table_pool.tile([P, Q_BLOCKS, 1, PAIRS, 2], BF16)
-            nc.sync.dma_start(out=q_table[:], in_=table_q[:, :, c : c + 1, :, :])
-            k_table = table_pool.tile([P, GROUPS, 2, PAIRS, 2], BF16)
-            nc.sync.dma_start(out=k_table[:], in_=table_k[:, :, 2 * c : 2 * c + 2, :, :])
-            return q_table, k_table
+        def load_table(c):
+            table = table_pool.tile([P, TABLE_ROWS, PAIRS, 2], BF16)
+            nc.sync.dma_start(out=table[:, 0:Q_BLOCKS], in_=table_q[:, :, c, :, :])
+            nc.sync.dma_start(
+                out=table[:, Q_BLOCKS:TABLE_ROWS].rearrange("p (g t) i e -> p g t i e", g=GROUPS),
+                in_=table_k[:, :, 2 * c : 2 * c + 2, :, :],
+            )
+            return table
+
+        def turn_table(table):
+            turned = turned_pool.tile([P, TABLE_ROWS, PAIRS, 2], BF16)
+            nc.scalar.mul(out=turned[:, :, :, 0], in_=table[:, :, :, 1], mul=-1.0)
+            nc.scalar.copy(out=turned[:, :, :, 1], in_=table[:, :, :, 0])
+            return turned
 
         def transpose_round(x_tile):
             words = x_tile[:].bitcast(F32)
@@ -117,8 +128,8 @@ def tile_causalselfattentiongqa_pa_t_kernel(
             return grouped
 
         def quantise(grouped):
-            codes = stage.tile([P, 2 * PASSES * P], U32, align_bytes=64)
-            scales = stage.tile([P, 2 * PASSES * P], U8, align_bytes=64)
+            codes = operand_pool.tile([P, 2 * PASSES * P], U32, align_bytes=64)
+            scales = operand_pool.tile([P, 2 * PASSES * P], U8, align_bytes=64)
             nc.vector.quantize_mx(
                 out=codes[:].bitcast(FP8X4),
                 scales=scales[:],
@@ -162,47 +173,48 @@ def tile_causalselfattentiongqa_pa_t_kernel(
                         )
             return q_banks, k_bank, v_bank
 
-        def rotate_bank(bank, table, straight, cross):
-            cos = table[:, :, :, :, 0:1].to_broadcast(list(bank.shape))
-            sin = table[:, :, :, :, 1]
-            nc.vector.tensor_tensor(out=straight, in0=bank, in1=cos, op=MULT)
-            nc.vector.scalar_tensor_tensor(
-                out=cross[:, 0], in0=bank[:, :, :, :, 1], scalar=-1.0, in1=sin, op0=MULT, op1=MULT
-            )
-            nc.vector.tensor_tensor(out=cross[:, 1], in0=bank[:, :, :, :, 0], in1=sin, op=MULT)
+        def rotate_bank(bank, table, turned, from_a, from_b):
+            shape = list(bank.shape)
+            nc.vector.tensor_tensor(out=from_a, in0=bank[:, :, :, :, 0:1].to_broadcast(shape), in1=table, op=MULT)
+            nc.vector.tensor_tensor(out=from_b, in0=bank[:, :, :, :, 1:2].to_broadcast(shape), in1=turned, op=MULT)
 
-        def rotate(banks, tables):
-            q_banks, k_bank, v_bank = banks
-            q_table, k_table = tables
-            straight = stage.tile([P, ROTATED, 2, PAIRS, 2], F32)
-            cross = stage.tile([P, 2, ROTATED, 2, PAIRS], F32)
+        def rotate(banks, table, turned):
+            q_banks, k_bank = banks[0], banks[1]
+            from_a = stage.tile([P, ROTATED, 2, PAIRS, 2], F32)
+            from_b = stage.tile([P, ROTATED, 2, PAIRS, 2], F32)
             for t in range(2):
                 rotate_bank(
                     q_banks[t][:].rearrange("p (b o i e) -> p b o i e", b=Q_BLOCKS, o=1, e=2),
-                    q_table[:],
-                    straight[:, 0:Q_BLOCKS, t : t + 1, :, :],
-                    cross[:, :, 0:Q_BLOCKS, t : t + 1, :],
+                    table[:, 0:Q_BLOCKS].rearrange("p (b o) i e -> p b o i e", o=1),
+                    turned[:, 0:Q_BLOCKS].rearrange("p (b o) i e -> p b o i e", o=1),
+                    from_a[:, 0:Q_BLOCKS, t : t + 1, :, :],
+                    from_b[:, 0:Q_BLOCKS, t : t + 1, :, :],
                 )
             rotate_bank(
                 k_bank[:].rearrange("p g t (i e) -> p g t i e", e=2),
-                k_table[:],
-                straight[:, Q_BLOCKS:ROTATED, :, :, :],
-                cross[:, :, Q_BLOCKS:ROTATED, :, :],
+                table[:, Q_BLOCKS:TABLE_ROWS].rearrange("p (g t) i e -> p g t i e", g=GROUPS),
+                turned[:, Q_BLOCKS:TABLE_ROWS].rearrange("p (g t) i e -> p g t i e", g=GROUPS),
+                from_a[:, Q_BLOCKS:ROTATED, :, :, :],
+                from_b[:, Q_BLOCKS:ROTATED, :, :, :],
             )
-            return straight, cross
+            return from_a, from_b
 
         x_tiles = [load_round(0), load_round(1)]
         load_weight()
-        tables = [load_tables(0)]
+        tables = [load_table(0)]
         for c in range(1, CHUNKS):
             x_tiles.append(load_round(2 * c))
             x_tiles.append(load_round(2 * c + 1))
-            tables.append(load_tables(c))
+            tables.append(load_table(c))
 
-        operands = {0: quantise(transpose_round(x_tiles[0]))}
+        grouped = {0: transpose_round(x_tiles[0])}
+        operands = {0: quantise(grouped[0])}
         gather_query_scales()
-        operands[1] = quantise(transpose_round(x_tiles[1]))
+        grouped[1] = transpose_round(x_tiles[1])
+        operands[1] = quantise(grouped[1])
+        turned = turn_table(tables[0])
         banks = {0: project(operands[0])}
+        grouped[2] = transpose_round(x_tiles[2])
         qk_out = None
         v_out = None
         for i in range(ROUNDS):
@@ -211,18 +223,18 @@ def tile_causalselfattentiongqa_pa_t_kernel(
                 qk_out = outs.tile([P, ROTATED, 2, 2, PAIRS, 2], F32)
                 v_out = outs.tile([P, GROUPS, 2, 2, HEAD], F32)
             nc.scalar.copy(out=v_out[:, :, :, r, :], in_=banks[i][2][:])
-            straight, cross = rotate(banks[i], tables[c])
-            grouped = transpose_round(x_tiles[i + 2]) if i + 2 < ROUNDS else None
+            from_a, from_b = rotate(banks[i], tables[c], turned)
+            if r == 1 and c + 1 < CHUNKS:
+                turned = turn_table(tables[c + 1])
+            if i + 3 < ROUNDS:
+                grouped[i + 3] = transpose_round(x_tiles[i + 3])
             if i + 1 < ROUNDS:
                 banks[i + 1] = project(operands[i + 1])
-            if i + 2 < ROUNDS:
-                operands[i + 2] = quantise(grouped)
-            nc.gpsimd.tensor_tensor(
-                out=qk_out[:, :, :, r, :, :],
-                in0=straight[:],
-                in1=cross[:].rearrange("p e b t i -> p b t i e"),
-                op=ADD,
-            )
+            if r == 0:
+                for n in range(i + 2, min(i + 4, ROUNDS)):
+                    operands[n] = quantise(grouped[n])
+            adder = nc.vector if i == ROUNDS - 1 else nc.gpsimd
+            adder.tensor_tensor(out=qk_out[:, :, :, r, :, :], in0=from_a[:], in1=from_b[:], op=ADD)
             if r == 1:
                 rows = slice(CHUNK * c, CHUNK * (c + 1))
                 nc.sync.dma_start(out=v_rows[:, :, rows, :], in_=v_out[:].rearrange("p g t r f -> p g (t r) f"))

@@ -25,13 +25,13 @@ PACK = 4
 K_PASS = P * PACK
 PASSES = C // K_PASS
 PASS_WORDS = K_PASS // 2
-CHUNK = 4
-CHUNKS = TOKENS // (P * CHUNK)
-ROUNDS = 2 * CHUNKS
+TILES = 2
+ROUNDS = TOKENS // (P * TILES)
 Q_BLOCKS = 4
 ROTATED = Q_BLOCKS + GROUPS
 Q_COLS = Q_BLOCKS * HEAD
-TABLE_ROWS = Q_BLOCKS + 2 * GROUPS
+TABLE_ROUNDS = 2
+TABLE_ROWS = Q_BLOCKS + GROUPS * TABLE_ROUNDS
 
 
 def tile_causalselfattentiongqa_pa_t_kernel(
@@ -52,11 +52,11 @@ def tile_causalselfattentiongqa_pa_t_kernel(
         ctx.enter_context(tc.manual_schedule())
         consts = ctx.enter_context(tc.tile_pool(name="consts", bufs=1))
         x_pool = ctx.enter_context(tc.tile_pool(name="x_pool", bufs=ROUNDS))
-        table_pool = ctx.enter_context(tc.tile_pool(name="table_pool", bufs=CHUNKS))
+        table_pool = ctx.enter_context(tc.tile_pool(name="table_pool", bufs=ROUNDS // TABLE_ROUNDS))
         turned_pool = ctx.enter_context(tc.tile_pool(name="turned_pool", bufs=2))
         stage = ctx.enter_context(tc.tile_pool(name="stage", bufs=3))
         operand_pool = ctx.enter_context(tc.tile_pool(name="operand_pool", bufs=4))
-        outs = ctx.enter_context(tc.tile_pool(name="outs", bufs=4))
+        outs = ctx.enter_context(tc.tile_pool(name="outs", bufs=8))
         psum_xt = ctx.enter_context(tc.psum_pool(name="psum_xt", bufs=2))
         psum_q = ctx.enter_context(tc.psum_pool(name="psum_q", bufs=3))
         psum_k = ctx.enter_context(tc.psum_pool(name="psum_k", bufs=2))
@@ -72,9 +72,9 @@ def tile_causalselfattentiongqa_pa_t_kernel(
         nc.vector.memset(w_scales[:].bitcast(I32), 0)
 
         def load_round(i):
-            c, r = divmod(i, 2)
-            x_tile = x_pool.tile([P, 2, C], BF16)
-            nc.sync.dma_start(out=x_tile[:], in_=x_rows[:, CHUNK * c + r : CHUNK * (c + 1) : 2, :])
+            x_tile = x_pool.tile([P, TILES, C], BF16)
+            for t in range(TILES):
+                nc.sync.dma_start(out=x_tile[:, t, :], in_=x_rows[:, TILES * i + t, :])
             return x_tile
 
         def load_weight():
@@ -101,8 +101,8 @@ def tile_causalselfattentiongqa_pa_t_kernel(
             table = table_pool.tile([P, TABLE_ROWS, PAIRS, 2], BF16)
             nc.sync.dma_start(out=table[:, 0:Q_BLOCKS], in_=table_q[:, :, c, :, :])
             nc.sync.dma_start(
-                out=table[:, Q_BLOCKS:TABLE_ROWS].rearrange("p (g t) i e -> p g t i e", g=GROUPS),
-                in_=table_k[:, :, 2 * c : 2 * c + 2, :, :],
+                out=table[:, Q_BLOCKS:TABLE_ROWS].rearrange("p (g r) i e -> p g r i e", g=GROUPS),
+                in_=table_k[:, :, TABLE_ROUNDS * c : TABLE_ROUNDS * (c + 1), :, :],
             )
             return table
 
@@ -114,8 +114,8 @@ def tile_causalselfattentiongqa_pa_t_kernel(
 
         def transpose_round(x_tile):
             words = x_tile[:].bitcast(F32)
-            grouped = stage.tile([P, 2, PASSES, P, PACK], BF16, align_bytes=64)
-            for t in range(2):
+            grouped = stage.tile([P, TILES, PASSES, P, PACK], BF16, align_bytes=64)
+            for t in range(TILES):
                 xt = psum_xt.tile([P, PASSES, 2, P], F32)
                 for h in range(PASSES):
                     for u in range(2):
@@ -128,8 +128,8 @@ def tile_causalselfattentiongqa_pa_t_kernel(
             return grouped
 
         def quantise(grouped):
-            codes = operand_pool.tile([P, 2 * PASSES * P], U32, align_bytes=64)
-            scales = operand_pool.tile([P, 2 * PASSES * P], U8, align_bytes=64)
+            codes = operand_pool.tile([P, TILES * PASSES * P], U32, align_bytes=64)
+            scales = operand_pool.tile([P, TILES * PASSES * P], U8, align_bytes=64)
             nc.vector.quantize_mx(
                 out=codes[:].bitcast(FP8X4),
                 scales=scales[:],
@@ -153,17 +153,17 @@ def tile_causalselfattentiongqa_pa_t_kernel(
 
         def project(operand):
             q_banks = []
-            for t in range(2):
+            for t in range(TILES):
                 q_bank = psum_q.tile([P, Q_COLS], F32)
                 multiply(q_bank[:], operand, t, lambda h: wq_words[:, h, :], lambda h: wq_scales[:, h, :])
                 q_banks.append(q_bank)
-            k_bank = psum_k.tile([P, GROUPS, 2, HEAD], F32)
-            v_bank = psum_v.tile([P, GROUPS, 2, HEAD], F32)
+            k_bank = psum_k.tile([P, GROUPS, TILES, HEAD], F32)
+            v_bank = psum_v.tile([P, GROUPS, TILES, HEAD], F32)
             for s, bank in ((0, k_bank), (1, v_bank)):
                 for g in range(GROUPS):
                     kv = 2 * g + s
                     col = (4 * g + 2 + s) * HEAD
-                    for t in range(2):
+                    for t in range(TILES):
                         multiply(
                             bank[:, g, t, :],
                             operand,
@@ -175,14 +175,18 @@ def tile_causalselfattentiongqa_pa_t_kernel(
 
         def rotate_bank(bank, table, turned, from_a, from_b):
             shape = list(bank.shape)
-            nc.vector.tensor_tensor(out=from_a, in0=bank[:, :, :, :, 0:1].to_broadcast(shape), in1=table, op=MULT)
-            nc.vector.tensor_tensor(out=from_b, in0=bank[:, :, :, :, 1:2].to_broadcast(shape), in1=turned, op=MULT)
+            nc.vector.tensor_tensor(
+                out=from_a, in0=bank[:, :, :, :, 0:1].to_broadcast(shape), in1=table.to_broadcast(shape), op=MULT
+            )
+            nc.vector.tensor_tensor(
+                out=from_b, in0=bank[:, :, :, :, 1:2].to_broadcast(shape), in1=turned.to_broadcast(shape), op=MULT
+            )
 
-        def rotate(banks, table, turned):
+        def rotate(banks, table, turned, r):
             q_banks, k_bank = banks[0], banks[1]
-            from_a = stage.tile([P, ROTATED, 2, PAIRS, 2], F32)
-            from_b = stage.tile([P, ROTATED, 2, PAIRS, 2], F32)
-            for t in range(2):
+            from_a = outs.tile([P, ROTATED, TILES, PAIRS, 2], F32)
+            from_b = stage.tile([P, ROTATED, TILES, PAIRS, 2], F32)
+            for t in range(TILES):
                 rotate_bank(
                     q_banks[t][:].rearrange("p (b o i e) -> p b o i e", b=Q_BLOCKS, o=1, e=2),
                     table[:, 0:Q_BLOCKS].rearrange("p (b o) i e -> p b o i e", o=1),
@@ -192,8 +196,8 @@ def tile_causalselfattentiongqa_pa_t_kernel(
                 )
             rotate_bank(
                 k_bank[:].rearrange("p g t (i e) -> p g t i e", e=2),
-                table[:, Q_BLOCKS:TABLE_ROWS].rearrange("p (g t) i e -> p g t i e", g=GROUPS),
-                turned[:, Q_BLOCKS:TABLE_ROWS].rearrange("p (g t) i e -> p g t i e", g=GROUPS),
+                table[:, Q_BLOCKS:TABLE_ROWS].rearrange("p (g r) i e -> p g r i e", g=GROUPS)[:, :, r : r + 1],
+                turned[:, Q_BLOCKS:TABLE_ROWS].rearrange("p (g r) i e -> p g r i e", g=GROUPS)[:, :, r : r + 1],
                 from_a[:, Q_BLOCKS:ROTATED, :, :, :],
                 from_b[:, Q_BLOCKS:ROTATED, :, :, :],
             )
@@ -202,9 +206,9 @@ def tile_causalselfattentiongqa_pa_t_kernel(
         x_tiles = [load_round(0), load_round(1)]
         load_weight()
         tables = [load_table(0)]
-        for c in range(1, CHUNKS):
-            x_tiles.append(load_round(2 * c))
-            x_tiles.append(load_round(2 * c + 1))
+        for c in range(1, ROUNDS // TABLE_ROUNDS):
+            for i in range(TABLE_ROUNDS * c, TABLE_ROUNDS * (c + 1)):
+                x_tiles.append(load_round(i))
             tables.append(load_table(c))
 
         grouped = {0: transpose_round(x_tiles[0])}
@@ -215,34 +219,27 @@ def tile_causalselfattentiongqa_pa_t_kernel(
         turned = turn_table(tables[0])
         banks = {0: project(operands[0])}
         grouped[2] = transpose_round(x_tiles[2])
-        qk_out = None
-        v_out = None
         for i in range(ROUNDS):
-            c, r = divmod(i, 2)
-            if r == 0:
-                qk_out = outs.tile([P, ROTATED, 2, 2, PAIRS, 2], F32)
-                v_out = outs.tile([P, GROUPS, 2, 2, HEAD], F32)
-            nc.scalar.copy(out=v_out[:, :, :, r, :], in_=banks[i][2][:])
-            from_a, from_b = rotate(banks[i], tables[c], turned)
-            if r == 1 and c + 1 < CHUNKS:
+            c, r = divmod(i, TABLE_ROUNDS)
+            v_out = outs.tile([P, GROUPS, TILES, HEAD], F32)
+            nc.scalar.copy(out=v_out[:], in_=banks[i][2][:])
+            from_a, from_b = rotate(banks[i], tables[c], turned, r)
+            if r == TABLE_ROUNDS - 1 and i + 1 < ROUNDS:
                 turned = turn_table(tables[c + 1])
             if i + 3 < ROUNDS:
                 grouped[i + 3] = transpose_round(x_tiles[i + 3])
             if i + 1 < ROUNDS:
                 banks[i + 1] = project(operands[i + 1])
-            if r == 0:
+            if i % 2 == 0:
                 for n in range(i + 2, min(i + 4, ROUNDS)):
                     operands[n] = quantise(grouped[n])
             adder = nc.vector if i == ROUNDS - 1 else nc.gpsimd
-            adder.tensor_tensor(out=qk_out[:, :, :, r, :, :], in0=from_a[:], in1=from_b[:], op=ADD)
-            if r == 1:
-                rows = slice(CHUNK * c, CHUNK * (c + 1))
-                nc.sync.dma_start(out=v_rows[:, :, rows, :], in_=v_out[:].rearrange("p g t r f -> p g (t r) f"))
-                nc.sync.dma_start(
-                    out=q_rows[:, :, rows, :],
-                    in_=qk_out[:, 0:Q_BLOCKS].rearrange("p b t r i e -> p b (t r) (i e)"),
-                )
-                nc.sync.dma_start(
-                    out=k_rows[:, :, rows, :],
-                    in_=qk_out[:, Q_BLOCKS:ROTATED].rearrange("p b t r i e -> p b (t r) (i e)"),
-                )
+            adder.tensor_tensor(out=from_a[:], in0=from_a[:], in1=from_b[:], op=ADD)
+            rows = slice(TILES * i, TILES * (i + 1))
+            nc.sync.dma_start(out=v_rows[:, :, rows, :], in_=v_out[:])
+            nc.sync.dma_start(
+                out=q_rows[:, :, rows, :], in_=from_a[:, 0:Q_BLOCKS].rearrange("p b t i e -> p b t (i e)")
+            )
+            nc.sync.dma_start(
+                out=k_rows[:, :, rows, :], in_=from_a[:, Q_BLOCKS:ROTATED].rearrange("p b t i e -> p b t (i e)")
+            )

@@ -30,6 +30,7 @@ ROUNDS = TOKENS // (P * TILES)
 Q_BLOCKS = 4
 ROTATED = Q_BLOCKS + GROUPS
 Q_COLS = Q_BLOCKS * HEAD
+ROUND_COLS = TILES * PASSES * P
 TABLE_ROUNDS = 2
 TABLE_ROWS = Q_BLOCKS + GROUPS * TABLE_ROUNDS
 
@@ -55,7 +56,7 @@ def tile_causalselfattentiongqa_pa_t_kernel(
         table_pool = ctx.enter_context(tc.tile_pool(name="table_pool", bufs=ROUNDS // TABLE_ROUNDS))
         turned_pool = ctx.enter_context(tc.tile_pool(name="turned_pool", bufs=2))
         stage = ctx.enter_context(tc.tile_pool(name="stage", bufs=3))
-        operand_pool = ctx.enter_context(tc.tile_pool(name="operand_pool", bufs=4))
+        operand_pool = ctx.enter_context(tc.tile_pool(name="operand_pool", bufs=3))
         outs = ctx.enter_context(tc.tile_pool(name="outs", bufs=8))
         psum_xt = ctx.enter_context(tc.psum_pool(name="psum_xt", bufs=2))
         psum_q = ctx.enter_context(tc.psum_pool(name="psum_q", bufs=3))
@@ -112,9 +113,15 @@ def tile_causalselfattentiongqa_pa_t_kernel(
             nc.scalar.copy(out=turned[:, :, :, 1], in_=table[:, :, :, 0])
             return turned
 
-        def transpose_round(x_tile):
+        def new_pair():
+            grouped = stage.tile([P, 2, TILES, PASSES, P, PACK], BF16, align_bytes=64)
+            codes = operand_pool.tile([P, 2 * TILES * PASSES * P], U32, align_bytes=64)
+            scales = operand_pool.tile([P, 2 * TILES * PASSES * P], U8, align_bytes=64)
+            return grouped, codes, scales
+
+        def transpose_round(x_tile, pair, r):
             words = x_tile[:].bitcast(F32)
-            grouped = stage.tile([P, TILES, PASSES, P, PACK], BF16, align_bytes=64)
+            grouped = pair[0]
             for t in range(TILES):
                 xt = psum_xt.tile([P, PASSES, 2, P], F32)
                 for h in range(PASSES):
@@ -124,23 +131,22 @@ def tile_causalselfattentiongqa_pa_t_kernel(
                             words[:, t, PASS_WORDS * h + u : PASS_WORDS * (h + 1) : 2],
                             ident[:],
                         )
-                nc.scalar.copy(out=grouped[:, t].bitcast(F32), in_=xt[:].rearrange("p h u n -> p h n u"))
-            return grouped
+                nc.scalar.copy(out=grouped[:, r, t].bitcast(F32), in_=xt[:].rearrange("p h u n -> p h n u"))
 
-        def quantise(grouped):
-            codes = operand_pool.tile([P, TILES * PASSES * P], U32, align_bytes=64)
-            scales = operand_pool.tile([P, TILES * PASSES * P], U8, align_bytes=64)
+        def quantise(pair, first, count):
+            grouped, codes, scales = pair
+            cols = slice(first * ROUND_COLS, (first + count) * ROUND_COLS)
             nc.vector.quantize_mx(
-                out=codes[:].bitcast(FP8X4),
-                scales=scales[:],
-                in_=grouped[:].rearrange("p t h n k -> p (t h n k)"),
+                out=codes[:, cols].bitcast(FP8X4),
+                scales=scales[:, cols],
+                in_=grouped[:, first : first + count].rearrange("p r t h n k -> p (r t h n k)"),
             )
-            return codes, scales
 
         def multiply(acc, operand, t, weight_words, weight_scales):
-            codes, scales = operand
+            (grouped, codes, scales), r = operand
             for h in range(PASSES):
-                cols = slice((PASSES * t + h) * P, (PASSES * t + h + 1) * P)
+                first = r * ROUND_COLS + (PASSES * t + h) * P
+                cols = slice(first, first + P)
                 nc.tensor.matmul_mx(
                     out=acc,
                     lhsT=codes[:, cols].bitcast(FP8X4),
@@ -211,14 +217,16 @@ def tile_causalselfattentiongqa_pa_t_kernel(
                 x_tiles.append(load_round(i))
             tables.append(load_table(c))
 
-        grouped = {0: transpose_round(x_tiles[0])}
-        operands = {0: quantise(grouped[0])}
+        pairs = {0: new_pair()}
+        transpose_round(x_tiles[0], pairs[0], 0)
+        quantise(pairs[0], 0, 1)
         gather_query_scales()
-        grouped[1] = transpose_round(x_tiles[1])
-        operands[1] = quantise(grouped[1])
+        transpose_round(x_tiles[1], pairs[0], 1)
+        quantise(pairs[0], 1, 1)
         turned = turn_table(tables[0])
-        banks = {0: project(operands[0])}
-        grouped[2] = transpose_round(x_tiles[2])
+        banks = {0: project((pairs[0], 0))}
+        pairs[1] = new_pair()
+        transpose_round(x_tiles[2], pairs[1], 0)
         for i in range(ROUNDS):
             c, r = divmod(i, TABLE_ROUNDS)
             v_out = outs.tile([P, GROUPS, TILES, HEAD], F32)
@@ -227,12 +235,13 @@ def tile_causalselfattentiongqa_pa_t_kernel(
             if r == TABLE_ROUNDS - 1 and i + 1 < ROUNDS:
                 turned = turn_table(tables[c + 1])
             if i + 3 < ROUNDS:
-                grouped[i + 3] = transpose_round(x_tiles[i + 3])
+                if (i + 3) % 2 == 0:
+                    pairs[(i + 3) // 2] = new_pair()
+                transpose_round(x_tiles[i + 3], pairs[(i + 3) // 2], (i + 3) % 2)
             if i + 1 < ROUNDS:
-                banks[i + 1] = project(operands[i + 1])
-            if i % 2 == 0:
-                for n in range(i + 2, min(i + 4, ROUNDS)):
-                    operands[n] = quantise(grouped[n])
+                banks[i + 1] = project((pairs[(i + 1) // 2], (i + 1) % 2))
+            if i % 2 == 0 and i + 2 < ROUNDS:
+                quantise(pairs[(i + 2) // 2], 0, 2)
             adder = nc.vector if i == ROUNDS - 1 else nc.gpsimd
             adder.tensor_tensor(out=from_a[:], in0=from_a[:], in1=from_b[:], op=ADD)
             rows = slice(TILES * i, TILES * (i + 1))

@@ -31,6 +31,7 @@ Q_BLOCKS = 4
 ROTATED = Q_BLOCKS + GROUPS
 Q_COLS = Q_BLOCKS * HEAD
 ROUND_COLS = TILES * PASSES * P
+SHARED_ROUNDS = ROUNDS - 3
 TABLE_ROUNDS = 2
 TABLE_ROWS = Q_BLOCKS + GROUPS * TABLE_ROUNDS
 
@@ -57,6 +58,7 @@ def tile_causalselfattentiongqa_pa_t_kernel(
         turned_pool = ctx.enter_context(tc.tile_pool(name="turned_pool", bufs=2))
         stage = ctx.enter_context(tc.tile_pool(name="stage", bufs=3))
         operand_pool = ctx.enter_context(tc.tile_pool(name="operand_pool", bufs=3))
+        gate_pool = ctx.enter_context(tc.tile_pool(name="gate_pool", bufs=2))
         outs = ctx.enter_context(tc.tile_pool(name="outs", bufs=8))
         psum_xt = ctx.enter_context(tc.psum_pool(name="psum_xt", bufs=2))
         psum_q = ctx.enter_context(tc.psum_pool(name="psum_q", bufs=3))
@@ -227,6 +229,7 @@ def tile_causalselfattentiongqa_pa_t_kernel(
         banks = {0: project((pairs[0], 0))}
         pairs[1] = new_pair()
         transpose_round(x_tiles[2], pairs[1], 0)
+        products = {}
         for i in range(ROUNDS):
             c, r = divmod(i, TABLE_ROUNDS)
             v_out = outs.tile([P, GROUPS, TILES, HEAD], F32)
@@ -240,15 +243,34 @@ def tile_causalselfattentiongqa_pa_t_kernel(
                 transpose_round(x_tiles[i + 3], pairs[(i + 3) // 2], (i + 3) % 2)
             if i + 1 < ROUNDS:
                 banks[i + 1] = project((pairs[(i + 1) // 2], (i + 1) % 2))
+            products[i] = (from_a, from_b)
+            shared = i < SHARED_ROUNDS
             if i % 2 == 0 and i + 2 < ROUNDS:
                 quantise(pairs[(i + 2) // 2], 0, 2)
+                for n in (i - 1, i):
+                    if n >= 0:
+                        a, b = products[n]
+                        nc.vector.tensor_tensor(
+                            out=a[:, ROTATED - 1], in0=a[:, ROTATED - 1], in1=b[:, ROTATED - 1], op=ADD
+                        )
+                gate = gate_pool.tile([P, 1], F32)
+                nc.gpsimd.tensor_copy(out=gate[:], in_=from_a[:, ROTATED - 1, 0, 0, 0:1])
             adder = nc.vector if i == ROUNDS - 1 else nc.gpsimd
-            adder.tensor_tensor(out=from_a[:], in0=from_a[:], in1=from_b[:], op=ADD)
+            mine = ROTATED - 1 if shared else ROTATED
+            adder.tensor_tensor(out=from_a[:, 0:mine], in0=from_a[:, 0:mine], in1=from_b[:, 0:mine], op=ADD)
+
+            def store_k(n):
+                nc.sync.dma_start(
+                    out=k_rows[:, :, TILES * n : TILES * (n + 1), :],
+                    in_=products[n][0][:, Q_BLOCKS:ROTATED].rearrange("p b t i e -> p b t (i e)"),
+                )
+
             rows = slice(TILES * i, TILES * (i + 1))
+            if shared and i % 2 == 0 and i > 0:
+                store_k(i - 1)
             nc.sync.dma_start(out=v_rows[:, :, rows, :], in_=v_out[:])
             nc.sync.dma_start(
                 out=q_rows[:, :, rows, :], in_=from_a[:, 0:Q_BLOCKS].rearrange("p b t i e -> p b t (i e)")
             )
-            nc.sync.dma_start(
-                out=k_rows[:, :, rows, :], in_=from_a[:, Q_BLOCKS:ROTATED].rearrange("p b t i e -> p b t (i e)")
-            )
+            if not (shared and i % 2 == 1):
+                store_k(i)

@@ -30,7 +30,8 @@ ROUNDS = TOKENS // (P * TILES)
 Q_BLOCKS = 4
 ROTATED = Q_BLOCKS + GROUPS
 Q_COLS = Q_BLOCKS * HEAD
-ROUND_COLS = TILES * PASSES * P
+TILE_COLS = PASSES * P
+WARM_UP = 4
 SHARED_ROUNDS = ROUNDS - 3
 TABLE_ROUNDS = 2
 TABLE_ROWS = Q_BLOCKS + GROUPS * TABLE_ROUNDS
@@ -68,29 +69,40 @@ def tile_causalselfattentiongqa_pa_t_kernel(
         ident = consts.tile([P, P], F32)
         make_identity(nc, ident[:])
 
+        zeros = consts.tile([P, Q_COLS], BF16)
+        nc.vector.memset(zeros[:], 0.0)
+        warm_bank = psum_q.tile([P, Q_COLS], F32, name="q_bank")
+        for n in range(WARM_UP):
+            nc.tensor.matmul(warm_bank[:], lhsT=zeros[:, 0:P], rhs=zeros[:], start=True, stop=True)
+
         wq_words = consts.tile([P, PASSES, 2 * Q_COLS], U8, align_bytes=64)
         wkv_words = consts.tile([P, PASSES, 2 * Q_COLS], U8, align_bytes=64)
         w_scales = consts.tile([P, PASSES, C], U8, align_bytes=64)
         wq_scales = consts.tile([P, PASSES, Q_COLS], U8, align_bytes=64)
         nc.vector.memset(w_scales[:].bitcast(I32), 0)
 
-        def load_round(i):
+        def load_tile(x_tile, i, t):
+            nc.sync.dma_start(out=x_tile[:, t, :], in_=x_rows[:, TILES * i + t, :])
+
+        def new_x_tile():
             x_tile = x_pool.tile([P, TILES, C], BF16)
-            for t in range(TILES):
-                nc.sync.dma_start(out=x_tile[:, t, :], in_=x_rows[:, TILES * i + t, :])
             return x_tile
 
-        def load_weight():
+        def load_round(i):
+            x_tile = new_x_tile()
+            for t in range(TILES):
+                load_tile(x_tile, i, t)
+            return x_tile
+
+        def load_weight_scales():
             for r in range(4):
                 nc.sync.dma_start(out=w_scales[r:P:32, :, :].bitcast(I32), in_=w_scale_rows[r])
+
+        def load_weight_words(words, first_slot):
             for h in range(PASSES):
                 nc.sync.dma_start(
-                    out=wq_words[:, h, :].bitcast(I32).rearrange("p (g s w) -> p g s w", g=GROUPS, s=2),
-                    in_=w_words[h][:, :, 0:2, :],
-                )
-                nc.sync.dma_start(
-                    out=wkv_words[:, h, :].bitcast(I32).rearrange("p (g s w) -> p g s w", g=GROUPS, s=2),
-                    in_=w_words[h][:, :, 2:4, :],
+                    out=words[:, h, :].bitcast(I32).rearrange("p (g s w) -> p g s w", g=GROUPS, s=2),
+                    in_=w_words[h][:, :, first_slot : first_slot + 2, :],
                 )
 
         def gather_query_scales():
@@ -102,52 +114,66 @@ def tile_causalselfattentiongqa_pa_t_kernel(
 
         def load_table(c):
             table = table_pool.tile([P, TABLE_ROWS, PAIRS, 2], BF16)
+            load_table_q(table, c)
+            load_table_k(table, c)
+            return table
+
+        def load_table_q(table, c):
             nc.sync.dma_start(out=table[:, 0:Q_BLOCKS], in_=table_q[:, :, c, :, :])
+
+        def load_table_k(table, c):
             nc.sync.dma_start(
                 out=table[:, Q_BLOCKS:TABLE_ROWS].rearrange("p (g r) i e -> p g r i e", g=GROUPS),
                 in_=table_k[:, :, TABLE_ROUNDS * c : TABLE_ROUNDS * (c + 1), :, :],
             )
-            return table
+
+        def turn_rows(turned, table, first, end):
+            nc.scalar.mul(out=turned[:, first:end, :, 0], in_=table[:, first:end, :, 1], mul=-1.0)
+            nc.scalar.copy(out=turned[:, first:end, :, 1], in_=table[:, first:end, :, 0])
 
         def turn_table(table):
             turned = turned_pool.tile([P, TABLE_ROWS, PAIRS, 2], BF16)
-            nc.scalar.mul(out=turned[:, :, :, 0], in_=table[:, :, :, 1], mul=-1.0)
-            nc.scalar.copy(out=turned[:, :, :, 1], in_=table[:, :, :, 0])
+            turn_rows(turned, table, 0, TABLE_ROWS)
             return turned
 
         def new_pair():
-            grouped = stage.tile([P, 2, TILES, PASSES, P, PACK], BF16, align_bytes=64)
-            codes = operand_pool.tile([P, 2 * TILES * PASSES * P], U32, align_bytes=64)
-            scales = operand_pool.tile([P, 2 * TILES * PASSES * P], U8, align_bytes=64)
+            grouped = stage.tile([P, 2 * TILES, PASSES, P, PACK], BF16, align_bytes=64)
+            codes = operand_pool.tile([P, 2 * TILES * TILE_COLS], U32, align_bytes=64)
+            scales = operand_pool.tile([P, 2 * TILES * TILE_COLS], U8, align_bytes=64)
             return grouped, codes, scales
 
-        def transpose_round(x_tile, pair, r):
-            words = x_tile[:].bitcast(F32)
-            grouped = pair[0]
-            for t in range(TILES):
-                xt = psum_xt.tile([P, PASSES, 2, P], F32)
-                for h in range(PASSES):
-                    for u in range(2):
-                        nc.tensor.transpose(
-                            xt[:, h, u, :],
-                            words[:, t, PASS_WORDS * h + u : PASS_WORDS * (h + 1) : 2],
-                            ident[:],
-                        )
-                nc.scalar.copy(out=grouped[:, r, t].bitcast(F32), in_=xt[:].rearrange("p h u n -> p h n u"))
+        def place(i, t):
+            return TILES * (i % 2) + t
 
-        def quantise(pair, first, count):
-            grouped, codes, scales = pair
-            cols = slice(first * ROUND_COLS, (first + count) * ROUND_COLS)
+        def transpose_tile(i, t):
+            words = x_tiles[i][:].bitcast(F32)
+            xt = psum_xt.tile([P, PASSES, 2, P], F32)
+            for h in range(PASSES):
+                for u in range(2):
+                    nc.tensor.transpose(
+                        xt[:, h, u, :], words[:, t, PASS_WORDS * h + u : PASS_WORDS * (h + 1) : 2], ident[:]
+                    )
+            nc.scalar.copy(
+                out=pairs[i // 2][0][:, place(i, t)].bitcast(F32), in_=xt[:].rearrange("p h u n -> p h n u")
+            )
+
+        def transpose_round(i):
+            for t in range(TILES):
+                transpose_tile(i, t)
+
+        def quantise(j, first, count):
+            grouped, codes, scales = pairs[j]
+            cols = slice(first * TILE_COLS, (first + count) * TILE_COLS)
             nc.vector.quantize_mx(
                 out=codes[:, cols].bitcast(FP8X4),
                 scales=scales[:, cols],
-                in_=grouped[:, first : first + count].rearrange("p r t h n k -> p (r t h n k)"),
+                in_=grouped[:, first : first + count].rearrange("p t h n k -> p (t h n k)"),
             )
 
-        def multiply(acc, operand, t, weight_words, weight_scales):
-            (grouped, codes, scales), r = operand
+        def multiply(acc, i, t, weight_words, weight_scales):
+            codes, scales = pairs[i // 2][1], pairs[i // 2][2]
             for h in range(PASSES):
-                first = r * ROUND_COLS + (PASSES * t + h) * P
+                first = place(i, t) * TILE_COLS + h * P
                 cols = slice(first, first + P)
                 nc.tensor.matmul_mx(
                     out=acc,
@@ -159,12 +185,13 @@ def tile_causalselfattentiongqa_pa_t_kernel(
                     stop=(h == PASSES - 1),
                 )
 
-        def project(operand):
-            q_banks = []
+        def project_q(i):
             for t in range(TILES):
                 q_bank = psum_q.tile([P, Q_COLS], F32)
-                multiply(q_bank[:], operand, t, lambda h: wq_words[:, h, :], lambda h: wq_scales[:, h, :])
-                q_banks.append(q_bank)
+                multiply(q_bank[:], i, t, lambda h: wq_words[:, h, :], lambda h: wq_scales[:, h, :])
+                q_banks[(i, t)] = q_bank
+
+        def project_kv(i):
             k_bank = psum_k.tile([P, GROUPS, TILES, HEAD], F32)
             v_bank = psum_v.tile([P, GROUPS, TILES, HEAD], F32)
             for s, bank in ((0, k_bank), (1, v_bank)):
@@ -174,12 +201,13 @@ def tile_causalselfattentiongqa_pa_t_kernel(
                     for t in range(TILES):
                         multiply(
                             bank[:, g, t, :],
-                            operand,
+                            i,
                             t,
                             lambda h: wkv_words[:, h, 2 * HEAD * kv : 2 * HEAD * (kv + 1)],
                             lambda h: w_scales[:, h, col : col + HEAD],
                         )
-            return q_banks, k_bank, v_bank
+            k_banks[i] = k_bank
+            v_banks[i] = v_bank
 
         def rotate_bank(bank, table, turned, from_a, from_b):
             shape = list(bank.shape)
@@ -190,87 +218,144 @@ def tile_causalselfattentiongqa_pa_t_kernel(
                 out=from_b, in0=bank[:, :, :, :, 1:2].to_broadcast(shape), in1=turned.to_broadcast(shape), op=MULT
             )
 
-        def rotate(banks, table, turned, r):
-            q_banks, k_bank = banks[0], banks[1]
+        def rotate_q(i, table, turned):
             from_a = outs.tile([P, ROTATED, TILES, PAIRS, 2], F32)
             from_b = stage.tile([P, ROTATED, TILES, PAIRS, 2], F32)
+            products[i] = (from_a, from_b)
             for t in range(TILES):
                 rotate_bank(
-                    q_banks[t][:].rearrange("p (b o i e) -> p b o i e", b=Q_BLOCKS, o=1, e=2),
+                    q_banks[(i, t)][:].rearrange("p (b o i e) -> p b o i e", b=Q_BLOCKS, o=1, e=2),
                     table[:, 0:Q_BLOCKS].rearrange("p (b o) i e -> p b o i e", o=1),
                     turned[:, 0:Q_BLOCKS].rearrange("p (b o) i e -> p b o i e", o=1),
                     from_a[:, 0:Q_BLOCKS, t : t + 1, :, :],
                     from_b[:, 0:Q_BLOCKS, t : t + 1, :, :],
                 )
+
+        def rotate_k(i, table, turned):
+            from_a, from_b = products[i]
+            r = i % TABLE_ROUNDS
             rotate_bank(
-                k_bank[:].rearrange("p g t (i e) -> p g t i e", e=2),
+                k_banks[i][:].rearrange("p g t (i e) -> p g t i e", e=2),
                 table[:, Q_BLOCKS:TABLE_ROWS].rearrange("p (g r) i e -> p g r i e", g=GROUPS)[:, :, r : r + 1],
                 turned[:, Q_BLOCKS:TABLE_ROWS].rearrange("p (g r) i e -> p g r i e", g=GROUPS)[:, :, r : r + 1],
                 from_a[:, Q_BLOCKS:ROTATED, :, :, :],
                 from_b[:, Q_BLOCKS:ROTATED, :, :, :],
             )
-            return from_a, from_b
 
-        x_tiles = [load_round(0), load_round(1)]
-        load_weight()
-        tables = [load_table(0)]
+        def copy_v(i):
+            v_out = outs.tile([P, GROUPS, TILES, HEAD], F32)
+            nc.scalar.copy(out=v_out[:], in_=v_banks[i][:])
+            nc.sync.dma_start(out=v_rows[:, :, TILES * i : TILES * (i + 1), :], in_=v_out[:])
+
+        def store_q(i):
+            nc.sync.dma_start(
+                out=q_rows[:, :, TILES * i : TILES * (i + 1), :],
+                in_=products[i][0][:, 0:Q_BLOCKS].rearrange("p b t i e -> p b t (i e)"),
+            )
+
+        def store_k(i):
+            nc.sync.dma_start(
+                out=k_rows[:, :, TILES * i : TILES * (i + 1), :],
+                in_=products[i][0][:, Q_BLOCKS:ROTATED].rearrange("p b t i e -> p b t (i e)"),
+            )
+
+        def add(engine, i, first, end):
+            from_a, from_b = products[i]
+            engine.tensor_tensor(out=from_a[:, first:end], in0=from_a[:, first:end], in1=from_b[:, first:end], op=ADD)
+
+        def quantise_and_add(i, j, first, count):
+            quantise(j, first, count)
+            for n in list(waiting):
+                if n <= i:
+                    add(nc.vector, n, ROTATED - 1, ROTATED)
+                    waiting.remove(n)
+                    summed.append(n)
+            gate = gate_pool.tile([P, 1], F32)
+            nc.gpsimd.tensor_copy(out=gate[:], in_=products[i][0][:, ROTATED - 1, 0, 0, 0:1])
+
+        def finish(i):
+            if i < SHARED_ROUNDS:
+                add(nc.gpsimd, i, 0, ROTATED - 1)
+            elif i + 1 < ROUNDS:
+                add(nc.gpsimd, i, 0, ROTATED)
+                summed.append(i)
+            else:
+                add(nc.vector, i, 0, ROTATED)
+                summed.append(i)
+            store_q(i)
+            for n in summed:
+                store_k(n)
+            summed.clear()
+
+        x_tiles = [new_x_tile()]
+        load_tile(x_tiles[0], 0, 0)
+        load_tile(x_tiles[0], 0, 1)
+        first_table = table_pool.tile([P, TABLE_ROWS, PAIRS, 2], BF16, name="table")
+        tables = [first_table]
+        load_table_q(first_table, 0)
+        load_weight_scales()
+        load_weight_words(wq_words, 0)
+        load_table_k(first_table, 0)
+        load_weight_words(wkv_words, 2)
+        x_tiles.append(load_round(1))
         for c in range(1, ROUNDS // TABLE_ROUNDS):
             for i in range(TABLE_ROUNDS * c, TABLE_ROUNDS * (c + 1)):
                 x_tiles.append(load_round(i))
             tables.append(load_table(c))
 
-        pairs = {0: new_pair()}
-        transpose_round(x_tiles[0], pairs[0], 0)
-        quantise(pairs[0], 0, 1)
+        pairs, q_banks, k_banks, v_banks, products = {}, {}, {}, {}, {}
+        waiting = list(range(SHARED_ROUNDS))
+        summed = []
+
+        pairs[0] = new_pair()
+        transpose_round(0)
+        quantise(0, 0, 1)
         gather_query_scales()
-        transpose_round(x_tiles[1], pairs[0], 1)
-        quantise(pairs[0], 1, 1)
-        turned = turn_table(tables[0])
-        banks = {0: project((pairs[0], 0))}
+        quantise(0, 1, 1)
+        turned = turned_pool.tile([P, TABLE_ROWS, PAIRS, 2], BF16)
+        turn_rows(turned, tables[0], 0, Q_BLOCKS)
+        turn_rows(turned, tables[0], Q_BLOCKS, TABLE_ROWS)
+        project_q(0)
+        transpose_round(1)
+        project_kv(0)
+
+        rotate_q(0, tables[0], turned)
+        quantise(0, TILES, TILES)
+        copy_v(0)
+        rotate_k(0, tables[0], turned)
         pairs[1] = new_pair()
-        transpose_round(x_tiles[2], pairs[1], 0)
-        products = {}
-        for i in range(ROUNDS):
+        transpose_round(2)
+        project_q(1)
+        project_kv(1)
+        quantise_and_add(0, 1, 0, TILES)
+        finish(0)
+
+        copy_v(1)
+        rotate_q(1, tables[0], turned)
+        rotate_k(1, tables[0], turned)
+        turned = turn_table(tables[1])
+        transpose_round(3)
+        project_q(2)
+        project_kv(2)
+        pairs[2] = new_pair()
+        transpose_round(4)
+        quantise_and_add(1, 1, TILES, TILES)
+        finish(1)
+
+        for i in range(2, ROUNDS):
             c, r = divmod(i, TABLE_ROUNDS)
-            v_out = outs.tile([P, GROUPS, TILES, HEAD], F32)
-            nc.scalar.copy(out=v_out[:], in_=banks[i][2][:])
-            from_a, from_b = rotate(banks[i], tables[c], turned, r)
+            copy_v(i)
+            rotate_q(i, tables[c], turned)
+            rotate_k(i, tables[c], turned)
             if r == TABLE_ROUNDS - 1 and i + 1 < ROUNDS:
                 turned = turn_table(tables[c + 1])
             if i + 3 < ROUNDS:
                 if (i + 3) % 2 == 0:
                     pairs[(i + 3) // 2] = new_pair()
-                transpose_round(x_tiles[i + 3], pairs[(i + 3) // 2], (i + 3) % 2)
+                transpose_round(i + 3)
             if i + 1 < ROUNDS:
-                banks[i + 1] = project((pairs[(i + 1) // 2], (i + 1) % 2))
-            products[i] = (from_a, from_b)
-            shared = i < SHARED_ROUNDS
+                project_q(i + 1)
+                project_kv(i + 1)
             if i % 2 == 0 and i + 2 < ROUNDS:
-                quantise(pairs[(i + 2) // 2], 0, 2)
-                for n in (i - 1, i):
-                    if n >= 0:
-                        a, b = products[n]
-                        nc.vector.tensor_tensor(
-                            out=a[:, ROTATED - 1], in0=a[:, ROTATED - 1], in1=b[:, ROTATED - 1], op=ADD
-                        )
-                gate = gate_pool.tile([P, 1], F32)
-                nc.gpsimd.tensor_copy(out=gate[:], in_=from_a[:, ROTATED - 1, 0, 0, 0:1])
-            adder = nc.vector if i == ROUNDS - 1 else nc.gpsimd
-            mine = ROTATED - 1 if shared else ROTATED
-            adder.tensor_tensor(out=from_a[:, 0:mine], in0=from_a[:, 0:mine], in1=from_b[:, 0:mine], op=ADD)
-
-            def store_k(n):
-                nc.sync.dma_start(
-                    out=k_rows[:, :, TILES * n : TILES * (n + 1), :],
-                    in_=products[n][0][:, Q_BLOCKS:ROTATED].rearrange("p b t i e -> p b t (i e)"),
-                )
-
-            rows = slice(TILES * i, TILES * (i + 1))
-            if shared and i % 2 == 0 and i > 0:
-                store_k(i - 1)
-            nc.sync.dma_start(out=v_rows[:, :, rows, :], in_=v_out[:])
-            nc.sync.dma_start(
-                out=q_rows[:, :, rows, :], in_=from_a[:, 0:Q_BLOCKS].rearrange("p b t i e -> p b t (i e)")
-            )
-            if not (shared and i % 2 == 1):
-                store_k(i)
+                quantise_and_add(i, (i + 2) // 2, 0, 2 * TILES)
+            finish(i)

from contextlib import ExitStack

import concourse.mybir as mybir
from concourse.masks import make_identity

FLOPS = 2 * 4096 * 1024 * 1024

F32 = mybir.dt.float32
BF16 = mybir.dt.bfloat16
I32 = mybir.dt.int32
U32 = mybir.dt.uint32
U8 = mybir.dt.uint8
FP8X4 = mybir.dt.float8_e4m3fn_x4
FP4X4 = mybir.dt.float4_e2m1fn_x4
MULT = mybir.AluOpType.mult
ADD = mybir.AluOpType.add

P = 128
TOKENS = 4096
C = 1024
HEAD = 128
PAIRS = HEAD // 2
GROUPS = 2
PACK = 4
K_PASS = P * PACK
PASSES = C // K_PASS
PASS_WORDS = K_PASS // 2
TILES = 2
ROUNDS = TOKENS // (P * TILES)
Q_BLOCKS = 4
ROTATED = Q_BLOCKS + GROUPS
Q_COLS = Q_BLOCKS * HEAD
TILE_COLS = PASSES * P
WARM_UP = 4
SHARED_ROUNDS = ROUNDS - 3
TABLE_ROUNDS = 2
TABLE_ROWS = Q_BLOCKS + GROUPS * TABLE_ROUNDS


def tile_causalselfattentiongqa_pa_t_kernel(
    tc, x, freqs_cis, W_attn_words, W_attn_scales, out_0, out_1, out_2
):
    nc = tc.nc

    x_rows = x.rearrange("o (p r) k -> p (o r) k", p=P)
    table_q = freqs_cis.rearrange("(b p c) i e -> p b c i e", b=Q_BLOCKS, p=P)
    table_k = freqs_cis.rearrange("(g p r) i e -> p g r i e", g=GROUPS, p=P)
    q_rows = out_0.rearrange("o n h f -> (o n h) f").rearrange("(b p r) f -> p b r f", b=Q_BLOCKS, p=P)
    k_rows = out_1.rearrange("o n h f -> (o n h) f").rearrange("(g p r) f -> p g r f", g=GROUPS, p=P)
    v_rows = out_2.rearrange("o n h f -> (o n h) f").rearrange("(g p r) f -> p g r f", g=GROUPS, p=P)
    w_words = W_attn_words.bitcast(I32).rearrange("h p (g s w) -> h p g s w", g=GROUPS, s=4)
    w_scale_rows = W_attn_scales.bitcast(I32).rearrange("h (q r) w -> r q h w", r=4)

    with ExitStack() as ctx:
        ctx.enter_context(tc.manual_schedule())
        consts = ctx.enter_context(tc.tile_pool(name="consts", bufs=1))
        x_pool = ctx.enter_context(tc.tile_pool(name="x_pool", bufs=ROUNDS))
        table_pool = ctx.enter_context(tc.tile_pool(name="table_pool", bufs=ROUNDS // TABLE_ROUNDS))
        turned_pool = ctx.enter_context(tc.tile_pool(name="turned_pool", bufs=2))
        stage = ctx.enter_context(tc.tile_pool(name="stage", bufs=3))
        operand_pool = ctx.enter_context(tc.tile_pool(name="operand_pool", bufs=3))
        gate_pool = ctx.enter_context(tc.tile_pool(name="gate_pool", bufs=2))
        outs = ctx.enter_context(tc.tile_pool(name="outs", bufs=8))
        psum_xt = ctx.enter_context(tc.psum_pool(name="psum_xt", bufs=2))
        psum_q = ctx.enter_context(tc.psum_pool(name="psum_q", bufs=3))
        psum_k = ctx.enter_context(tc.psum_pool(name="psum_k", bufs=2))
        psum_v = ctx.enter_context(tc.psum_pool(name="psum_v", bufs=1))

        ident = consts.tile([P, P], F32)
        make_identity(nc, ident[:])

        zeros = consts.tile([P, Q_COLS], BF16)
        nc.vector.memset(zeros[:], 0.0)
        warm_bank = psum_q.tile([P, Q_COLS], F32, name="q_bank")
        for n in range(WARM_UP):
            nc.tensor.matmul(warm_bank[:], lhsT=zeros[:, 0:P], rhs=zeros[:], start=True, stop=True)

        wq_words = consts.tile([P, PASSES, 2 * Q_COLS], U8, align_bytes=64)
        wkv_words = consts.tile([P, PASSES, 2 * Q_COLS], U8, align_bytes=64)
        w_scales = consts.tile([P, PASSES, C], U8, align_bytes=64)
        wq_scales = consts.tile([P, PASSES, Q_COLS], U8, align_bytes=64)
        nc.vector.memset(w_scales[:].bitcast(I32), 0)

        def load_tile(x_tile, i, t):
            nc.sync.dma_start(out=x_tile[:, t, :], in_=x_rows[:, TILES * i + t, :])

        def new_x_tile():
            x_tile = x_pool.tile([P, TILES, C], BF16)
            return x_tile

        def load_round(i):
            x_tile = new_x_tile()
            for t in range(TILES):
                load_tile(x_tile, i, t)
            return x_tile

        def load_weight_scales():
            for r in range(4):
                nc.sync.dma_start(out=w_scales[r:P:32, :, :].bitcast(I32), in_=w_scale_rows[r])

        def load_weight_words(words, first_slot):
            for h in range(PASSES):
                nc.sync.dma_start(
                    out=words[:, h, :].bitcast(I32).rearrange("p (g s w) -> p g s w", g=GROUPS, s=2),
                    in_=w_words[h][:, :, first_slot : first_slot + 2, :],
                )

        def gather_query_scales():
            by_group = w_scales[:].bitcast(I32).rearrange("p h (g w) -> p h g w", g=GROUPS)
            nc.vector.tensor_copy(
                out=wq_scales[:].bitcast(I32).rearrange("p h (g w) -> p h g w", g=GROUPS),
                in_=by_group[:, :, :, 0 : Q_COLS // GROUPS // 4],
            )

        def load_table(c):
            table = table_pool.tile([P, TABLE_ROWS, PAIRS, 2], BF16)
            load_table_q(table, c)
            load_table_k(table, c)
            return table

        def load_table_q(table, c):
            nc.sync.dma_start(out=table[:, 0:Q_BLOCKS], in_=table_q[:, :, c, :, :])

        def load_table_k(table, c):
            nc.sync.dma_start(
                out=table[:, Q_BLOCKS:TABLE_ROWS].rearrange("p (g r) i e -> p g r i e", g=GROUPS),
                in_=table_k[:, :, TABLE_ROUNDS * c : TABLE_ROUNDS * (c + 1), :, :],
            )

        def turn_rows(turned, table, first, end):
            nc.scalar.mul(out=turned[:, first:end, :, 0], in_=table[:, first:end, :, 1], mul=-1.0)
            nc.scalar.copy(out=turned[:, first:end, :, 1], in_=table[:, first:end, :, 0])

        def turn_table(table):
            turned = turned_pool.tile([P, TABLE_ROWS, PAIRS, 2], BF16)
            turn_rows(turned, table, 0, TABLE_ROWS)
            return turned

        def new_pair():
            grouped = stage.tile([P, 2 * TILES, PASSES, P, PACK], BF16, align_bytes=64)
            codes = operand_pool.tile([P, 2 * TILES * TILE_COLS], U32, align_bytes=64)
            scales = operand_pool.tile([P, 2 * TILES * TILE_COLS], U8, align_bytes=64)
            return grouped, codes, scales

        def place(i, t):
            return TILES * (i % 2) + t

        def transpose_tile(i, t):
            words = x_tiles[i][:].bitcast(F32)
            xt = psum_xt.tile([P, PASSES, 2, P], F32)
            for h in range(PASSES):
                for u in range(2):
                    nc.tensor.transpose(
                        xt[:, h, u, :], words[:, t, PASS_WORDS * h + u : PASS_WORDS * (h + 1) : 2], ident[:]
                    )
            nc.scalar.copy(
                out=pairs[i // 2][0][:, place(i, t)].bitcast(F32), in_=xt[:].rearrange("p h u n -> p h n u")
            )

        def transpose_round(i):
            for t in range(TILES):
                transpose_tile(i, t)

        def quantise(j, first, count):
            grouped, codes, scales = pairs[j]
            cols = slice(first * TILE_COLS, (first + count) * TILE_COLS)
            nc.vector.quantize_mx(
                out=codes[:, cols].bitcast(FP8X4),
                scales=scales[:, cols],
                in_=grouped[:, first : first + count].rearrange("p t h n k -> p (t h n k)"),
            )

        def multiply(acc, i, t, weight_words, weight_scales):
            codes, scales = pairs[i // 2][1], pairs[i // 2][2]
            for h in range(PASSES):
                first = place(i, t) * TILE_COLS + h * P
                cols = slice(first, first + P)
                nc.tensor.matmul_mx(
                    out=acc,
                    lhsT=codes[:, cols].bitcast(FP8X4),
                    lhsT_scale=scales[:, cols],
                    rhs=weight_words(h).bitcast(FP4X4),
                    rhs_scale=weight_scales(h),
                    start=(h == 0),
                    stop=(h == PASSES - 1),
                )

        def project_q(i):
            for t in range(TILES):
                q_bank = psum_q.tile([P, Q_COLS], F32)
                multiply(q_bank[:], i, t, lambda h: wq_words[:, h, :], lambda h: wq_scales[:, h, :])
                q_banks[(i, t)] = q_bank

        def project_kv(i):
            k_bank = psum_k.tile([P, GROUPS, TILES, HEAD], F32)
            v_bank = psum_v.tile([P, GROUPS, TILES, HEAD], F32)
            for s, bank in ((0, k_bank), (1, v_bank)):
                for g in range(GROUPS):
                    kv = 2 * g + s
                    col = (4 * g + 2 + s) * HEAD
                    for t in range(TILES):
                        multiply(
                            bank[:, g, t, :],
                            i,
                            t,
                            lambda h: wkv_words[:, h, 2 * HEAD * kv : 2 * HEAD * (kv + 1)],
                            lambda h: w_scales[:, h, col : col + HEAD],
                        )
            k_banks[i] = k_bank
            v_banks[i] = v_bank

        def rotate_bank(bank, table, turned, from_a, from_b):
            shape = list(bank.shape)
            nc.vector.tensor_tensor(
                out=from_a, in0=bank[:, :, :, :, 0:1].to_broadcast(shape), in1=table.to_broadcast(shape), op=MULT
            )
            nc.vector.tensor_tensor(
                out=from_b, in0=bank[:, :, :, :, 1:2].to_broadcast(shape), in1=turned.to_broadcast(shape), op=MULT
            )

        def rotate_q(i, table, turned):
            from_a = outs.tile([P, ROTATED, TILES, PAIRS, 2], F32)
            from_b = stage.tile([P, ROTATED, TILES, PAIRS, 2], F32)
            products[i] = (from_a, from_b)
            for t in range(TILES):
                rotate_bank(
                    q_banks[(i, t)][:].rearrange("p (b o i e) -> p b o i e", b=Q_BLOCKS, o=1, e=2),
                    table[:, 0:Q_BLOCKS].rearrange("p (b o) i e -> p b o i e", o=1),
                    turned[:, 0:Q_BLOCKS].rearrange("p (b o) i e -> p b o i e", o=1),
                    from_a[:, 0:Q_BLOCKS, t : t + 1, :, :],
                    from_b[:, 0:Q_BLOCKS, t : t + 1, :, :],
                )

        def rotate_k(i, table, turned):
            from_a, from_b = products[i]
            r = i % TABLE_ROUNDS
            rotate_bank(
                k_banks[i][:].rearrange("p g t (i e) -> p g t i e", e=2),
                table[:, Q_BLOCKS:TABLE_ROWS].rearrange("p (g r) i e -> p g r i e", g=GROUPS)[:, :, r : r + 1],
                turned[:, Q_BLOCKS:TABLE_ROWS].rearrange("p (g r) i e -> p g r i e", g=GROUPS)[:, :, r : r + 1],
                from_a[:, Q_BLOCKS:ROTATED, :, :, :],
                from_b[:, Q_BLOCKS:ROTATED, :, :, :],
            )

        def copy_v(i):
            v_out = outs.tile([P, GROUPS, TILES, HEAD], F32)
            nc.scalar.copy(out=v_out[:], in_=v_banks[i][:])
            nc.sync.dma_start(out=v_rows[:, :, TILES * i : TILES * (i + 1), :], in_=v_out[:])

        def store_q(i):
            nc.sync.dma_start(
                out=q_rows[:, :, TILES * i : TILES * (i + 1), :],
                in_=products[i][0][:, 0:Q_BLOCKS].rearrange("p b t i e -> p b t (i e)"),
            )

        def store_k(i):
            nc.sync.dma_start(
                out=k_rows[:, :, TILES * i : TILES * (i + 1), :],
                in_=products[i][0][:, Q_BLOCKS:ROTATED].rearrange("p b t i e -> p b t (i e)"),
            )

        def add(engine, i, first, end):
            from_a, from_b = products[i]
            engine.tensor_tensor(out=from_a[:, first:end], in0=from_a[:, first:end], in1=from_b[:, first:end], op=ADD)

        def quantise_and_add(i, j, first, count):
            quantise(j, first, count)
            for n in list(waiting):
                if n <= i:
                    add(nc.vector, n, ROTATED - 1, ROTATED)
                    waiting.remove(n)
                    summed.append(n)
            gate = gate_pool.tile([P, 1], F32)
            nc.gpsimd.tensor_copy(out=gate[:], in_=products[i][0][:, ROTATED - 1, 0, 0, 0:1])

        def finish(i):
            if i < SHARED_ROUNDS:
                add(nc.gpsimd, i, 0, ROTATED - 1)
            elif i + 1 < ROUNDS:
                add(nc.gpsimd, i, 0, ROTATED)
                summed.append(i)
            else:
                add(nc.vector, i, 0, ROTATED)
                summed.append(i)
            store_q(i)
            for n in summed:
                store_k(n)
            summed.clear()

        x_tiles = [new_x_tile()]
        load_tile(x_tiles[0], 0, 0)
        load_tile(x_tiles[0], 0, 1)
        first_table = table_pool.tile([P, TABLE_ROWS, PAIRS, 2], BF16, name="table")
        tables = [first_table]
        load_table_q(first_table, 0)
        load_weight_scales()
        load_weight_words(wq_words, 0)
        load_table_k(first_table, 0)
        load_weight_words(wkv_words, 2)
        x_tiles.append(load_round(1))
        for c in range(1, ROUNDS // TABLE_ROUNDS):
            for i in range(TABLE_ROUNDS * c, TABLE_ROUNDS * (c + 1)):
                x_tiles.append(load_round(i))
            tables.append(load_table(c))

        pairs, q_banks, k_banks, v_banks, products = {}, {}, {}, {}, {}
        waiting = list(range(SHARED_ROUNDS))
        summed = []

        pairs[0] = new_pair()
        transpose_round(0)
        quantise(0, 0, 1)
        gather_query_scales()
        quantise(0, 1, 1)
        turned = turned_pool.tile([P, TABLE_ROWS, PAIRS, 2], BF16)
        turn_rows(turned, tables[0], 0, Q_BLOCKS)
        turn_rows(turned, tables[0], Q_BLOCKS, TABLE_ROWS)
        project_q(0)
        transpose_round(1)
        project_kv(0)

        rotate_q(0, tables[0], turned)
        quantise(0, TILES, TILES)
        copy_v(0)
        rotate_k(0, tables[0], turned)
        pairs[1] = new_pair()
        transpose_round(2)
        project_q(1)
        project_kv(1)
        quantise_and_add(0, 1, 0, TILES)
        finish(0)

        copy_v(1)
        rotate_q(1, tables[0], turned)
        rotate_k(1, tables[0], turned)
        turned = turn_table(tables[1])
        transpose_round(3)
        project_q(2)
        project_kv(2)
        pairs[2] = new_pair()
        transpose_round(4)
        quantise_and_add(1, 1, TILES, TILES)
        finish(1)

        for i in range(2, ROUNDS):
            c, r = divmod(i, TABLE_ROUNDS)
            copy_v(i)
            rotate_q(i, tables[c], turned)
            rotate_k(i, tables[c], turned)
            if r == TABLE_ROUNDS - 1 and i + 1 < ROUNDS:
                turned = turn_table(tables[c + 1])
            if i + 3 < ROUNDS:
                if (i + 3) % 2 == 0:
                    pairs[(i + 3) // 2] = new_pair()
                transpose_round(i + 3)
            if i + 1 < ROUNDS:
                project_q(i + 1)
                project_kv(i + 1)
            if i % 2 == 0 and i + 2 < ROUNDS:
                quantise_and_add(i, (i + 2) // 2, 0, 2 * TILES)
            finish(i)
